import numpy as np
import ml_dtypes


def mxq(x, axis, fmt="e4m3"):
    dtype, down = {"e4m3": (ml_dtypes.float8_e4m3fn, 7), "e5m2": (ml_dtypes.float8_e5m2, 14)}[fmt]
    v = np.moveaxis(np.asarray(x, np.float32).astype(ml_dtypes.bfloat16).astype(np.float64), axis, -1)
    blocks = v.reshape(v.shape[:-1] + (-1, 32))
    amax = np.abs(blocks).max(-1, keepdims=True)
    byte = np.maximum(np.where(amax > 0, np.frexp(amax)[1] - 1 + 127, 0) - down, 1)
    scale = np.exp2(byte - 127.0)
    codes = (blocks / scale).astype(np.float32).astype(dtype).astype(np.float64)
    return np.moveaxis((codes * scale).reshape(v.shape), -1, axis)


WIDE = False


def mx_kscale(k):
    if not WIDE:
        return np.ones(k)
    levels = np.array([30, -30])
    if k % 512:
        return np.exp2(np.random.permutation(np.resize(levels, k // 32))).repeat(32)
    a = np.empty((k // 512, 16))
    for p in range(k // 512):
        a[p, :8] = np.random.permutation(np.resize(levels, 8))
        for g in range(8):
            far = levels[np.abs(levels - a[p, g]) >= 10]
            a[p, g + 8] = far[np.random.randint(len(far))]
    return np.exp2(a.ravel()).repeat(32)


BF16 = ml_dtypes.bfloat16


def bf(x):
    return np.asarray(x, np.float32).astype(BF16)


def f64(x):
    return np.asarray(x).astype(np.float64)


B, L, D, H, QK, V = 4, 512, 1024, 8, 128, 128


def rotate_by_i(x):
    x2 = x.reshape(x.shape[:-1] + (-1, 2))
    real, imag = x2[..., 0], x2[..., 1]
    return np.stack([-imag, real], axis=-1).reshape(x.shape)


def setup_inputs():
    s = mx_kscale(D)
    a = np.random.uniform(-np.pi, np.pi, (B, L, QK // 2))
    return {"sequence": bf(np.random.standard_normal((B, L, D)) * s),
            "w_q": bf(np.random.standard_normal((H, D, QK)) * 0.3 / np.sqrt(D) / s[:, None]),
            "w_k": bf(np.random.standard_normal((H, D, QK)) * 0.3 / np.sqrt(D) / s[:, None]),
            "cos_half": bf(np.cos(a)), "sin_half": bf(np.sin(a))}


def reference(sequence, w_q, w_k, cos_half, sin_half):
    xq = mxq(f64(sequence), 2, "e5m2")[None]
    q = xq @ mxq(f64(w_q), 1, "e4m3")[:, None]
    k = xq @ mxq(f64(w_k), 1, "e4m3")[:, None]
    cos = np.repeat(f64(cos_half), 2, axis=-1)
    sin = np.repeat(f64(sin_half), 2, axis=-1)
    q_rot = cos * q + sin * rotate_by_i(q)
    k_rot = cos * k - sin * rotate_by_i(k)
    return q_rot, k_rot

@@ -1,0 +1,247 @@
+from contextlib import ExitStack
+
+import concourse.mybir as mybir
+from concourse.masks import make_identity
+
+B, L, D, H, QK = 4, 512, 1024, 8, 128
+T = B * L
+FLOPS = 2 * T * D * 2 * H * QK
+
+F32 = mybir.dt.float32
+BF16 = mybir.dt.bfloat16
+U32 = mybir.dt.uint32
+U8 = mybir.dt.uint8
+E5M2 = mybir.dt.float8_e5m2_x4
+E4M3 = mybir.dt.float8_e4m3fn_x4
+ALU = mybir.AluOpType
+
+P = 128
+PACK = 4
+PASSES = D // (P * PACK)
+SLOTS = T // P
+GROUP = 4
+GROUPS = SLOTS // GROUP
+HEADS = 4
+SETS = 2 * H // HEADS
+PAIRS = QK // 2
+
+
+def tile_multiscaleretention_pa_kernel(tc, sequence, w_q, w_k, cos_half, sin_half, out_0, out_1):
+    nc = tc.nc
+    x_hbm = sequence.rearrange("b l d -> (b l) d").rearrange("(p s) d -> p s d", p=P)
+    cos_hbm = cos_half.rearrange("b l i -> (b l) i").rearrange("(p s) i -> p s i", p=P)
+    sin_hbm = sin_half.rearrange("b l i -> (b l) i").rearrange("(p s) i -> p s i", p=P)
+
+    def set_weights(c):
+        return (w_q, w_k)[c // 2][(c % 2) * HEADS : (c % 2 + 1) * HEADS]
+
+    def set_output(c):
+        heads = (out_0, out_1)[c // 2][(c % 2) * HEADS : (c % 2 + 1) * HEADS]
+        return heads.rearrange("h b l c -> h (b l) c").rearrange("h (p s) c -> p h s c", p=P)
+
+    with ExitStack() as ctx:
+        keep = ctx.enter_context(tc.tile_pool(name="keep", bufs=1))
+        stage = ctx.enter_context(tc.tile_pool(name="stage", bufs=2))
+        prod = ctx.enter_context(tc.tile_pool(name="prod", bufs=3))
+        res = ctx.enter_context(tc.tile_pool(name="res", bufs=3))
+        psum_t = ctx.enter_context(tc.psum_pool(name="psum_t", bufs=2))
+        psum_m = ctx.enter_context(tc.psum_pool(name="psum_m", bufs=6))
+        ctx.enter_context(tc.manual_schedule())
+
+        x_raw = keep.tile([P, SLOTS, D], BF16, align_bytes=64)
+        w_raw = keep.tile([P, SETS, PASSES, HEADS, PACK, QK], BF16, align_bytes=64)
+        cos_sb = keep.tile([P, SLOTS, PAIRS], BF16, align_bytes=64)
+        sin_sb = keep.tile([P, SLOTS, PAIRS], BF16, align_bytes=64)
+        sin_signed = keep.tile([P, SLOTS, PAIRS, 2], BF16, align_bytes=64)
+        signs = keep.tile([P, 2], F32)
+        ident = keep.tile([P, P], F32)
+        x_codes = keep.tile([P, GROUPS, PASSES, GROUP * P], U32, align_bytes=64)
+        x_scales = keep.tile([P, GROUPS, PASSES, GROUP * P], U8, align_bytes=64)
+        w_codes = keep.tile([P, SETS, PASSES, HEADS * QK], U32, align_bytes=64)
+        w_scales = keep.tile([P, SETS, PASSES, HEADS * QK], U8, align_bytes=64)
+
+        def load_x(s0, s1):
+            nc.sync.dma_start(out=x_raw[:, s0:s1, :], in_=x_hbm[:, s0:s1, :])
+
+        def load_w(c, g):
+            rows = set_weights(c)[:, g * P * PACK : (g + 1) * P * PACK, :]
+            nc.sync.dma_start(
+                out=w_raw[:, c, g].rearrange("p h t c -> p h (t c)"),
+                in_=rows.rearrange("h (p t) c -> p h (t c)", t=PACK),
+            )
+
+        load_x(0, 1)
+        nc.sync.dma_start(out=sin_sb[:], in_=sin_hbm)
+        load_w(0, 0)
+        load_w(0, 1)
+        nc.sync.dma_start(out=cos_sb[:], in_=cos_hbm)
+        load_x(1, GROUP)
+        for r in range(1, GROUPS):
+            load_x(r * GROUP, (r + 1) * GROUP)
+        for c in range(1, SETS):
+            for g in range(PASSES):
+                load_w(c, g)
+
+        make_identity(nc, ident[:])
+        nc.vector.memset(signs[:, 0:1], -1.0)
+        nc.vector.memset(signs[:, 1:2], 1.0)
+
+        x_packed = {}
+        w_packed = {}
+
+        def transpose_x(r, j):
+            if j == 0:
+                x_packed[r] = stage.tile([P, PASSES, GROUP, P, PACK], BF16, align_bytes=64, name="x_packed")
+            words = x_raw[:, r * GROUP + j, :].bitcast(F32)
+            bank = psum_t.tile([P, PASSES, 2, P], F32, name="bank_t")
+            for g in range(PASSES):
+                for u in range(2):
+                    nc.tensor.transpose(bank[:, g, u, :], words[:, 2 * P * g + u : 2 * P * (g + 1) : 2], ident[:])
+            dst = x_packed[r][:, :, j].rearrange("p g m t -> p g (m t)").bitcast(F32)
+            nc.scalar.copy(
+                out=dst.rearrange("p g (m u) -> p g m u", u=2),
+                in_=bank[:].rearrange("p g u m -> p g m u"),
+            )
+
+        def quantize_x(r, g, j0, j1):
+            nc.vector.quantize_mx(
+                out=x_codes[:, r, g, j0 * P : j1 * P].bitcast(E5M2),
+                scales=x_scales[:, r, g, j0 * P : j1 * P],
+                in_=x_packed[r][:, g, j0:j1].rearrange("p j m t -> p (j m t)"),
+            )
+
+        def quantize_x_group(r):
+            nc.vector.quantize_mx(
+                out=x_codes[:, r].rearrange("p g m -> p (g m)").bitcast(E5M2),
+                scales=x_scales[:, r].rearrange("p g m -> p (g m)"),
+                in_=x_packed[r][:].rearrange("p g j m t -> p (g j m t)"),
+            )
+
+        def pack_w(c, g, h, on_vector=False):
+            if c not in w_packed:
+                w_packed[c] = stage.tile([P, PASSES, HEADS, QK, PACK], BF16, align_bytes=64, name="w_packed")
+            dst = w_packed[c][:, g, h].rearrange("p (n i) t -> p n t i", i=4)
+            src = w_raw[:, c, g, h].rearrange("p t (n i) -> p n t i", i=4)
+            if on_vector:
+                nc.vector.tensor_copy(out=dst, in_=src)
+            else:
+                nc.scalar.copy(out=dst, in_=src)
+
+        def quantize_w(c, g):
+            nc.vector.quantize_mx(
+                out=w_codes[:, c, g].bitcast(E4M3),
+                scales=w_scales[:, c, g],
+                in_=w_packed[c][:, g].rearrange("p h n t -> p (h n t)"),
+            )
+
+        def multiply(c, r, j):
+            acc = psum_m.tile([P, HEADS * QK], F32, name="acc")
+            for g in range(PASSES):
+                nc.tensor.matmul_mx(
+                    out=acc[:],
+                    lhsT=x_codes[:, r, g, j * P : (j + 1) * P].bitcast(E5M2),
+                    lhsT_scale=x_scales[:, r, g, j * P : (j + 1) * P],
+                    rhs=w_codes[:, c, g].bitcast(E4M3),
+                    rhs_scale=w_scales[:, c, g],
+                    start=(g == 0),
+                    stop=(g == PASSES - 1),
+                )
+            return acc
+
+        shape4 = [P, HEADS, PAIRS, 2]
+
+        def products(acc, s, cos_part, sin_part):
+            pairs = acc[:].rearrange("p (h i e) -> p h i e", h=HEADS, e=2)
+            nc.vector.tensor_tensor(
+                out=cos_part.rearrange("p h (i e) -> p h i e", e=2),
+                in0=pairs,
+                in1=cos_sb[:, s, :].unsqueeze(1).unsqueeze(3).to_broadcast(shape4),
+                op=ALU.mult,
+            )
+            nc.vector.tensor_tensor(
+                out=sin_part.rearrange("p h (i e) -> p h i e", e=2),
+                in0=pairs[:, :, :, ::-1],
+                in1=sin_signed[:, s].unsqueeze(1).to_broadcast(shape4),
+                op=ALU.mult,
+            )
+
+        transpose_x(0, 0)
+        nc.vector.tensor_tensor(
+            out=sin_signed[:].rearrange("p s i e -> p (s i) e"),
+            in0=sin_sb[:].rearrange("p s i -> p (s i)").unsqueeze(2).to_broadcast([P, SLOTS * PAIRS, 2]),
+            in1=signs[:].unsqueeze(1).to_broadcast([P, SLOTS * PAIRS, 2]),
+            op=ALU.mult,
+        )
+        pack_w(0, 0, 0)
+        for h in range(1, HEADS):
+            pack_w(0, 0, h, on_vector=True)
+        for g in range(PASSES):
+            quantize_x(0, g, 0, 1)
+        quantize_w(0, 0)
+        pack_w(0, 1, 0)
+        pack_w(0, 1, 1)
+        pack_w(0, 1, 2, on_vector=True)
+        pack_w(0, 1, 3, on_vector=True)
+        transpose_x(0, 1)
+        quantize_w(0, 1)
+
+        steps = [(c, r) for c in range(SETS) for r in range(GROUPS)]
+        accs = {(0, 0): multiply(0, 0, 0)}
+        transpose_x(0, 2)
+        transpose_x(0, 3)
+
+        for n, (c, r) in enumerate(steps):
+            last = n == len(steps) - 1
+            result = res.tile([P, HEADS, GROUP, QK], F32, name="result")
+            op = ALU.add if c < SETS // 2 else ALU.subtract
+            for half in range(2):
+                cos_part = prod.tile([P, 2, HEADS, QK], F32, name="cos_part")
+                sin_part = prod.tile([P, 2, HEADS, QK], F32, name="sin_part")
+                for jj in range(2):
+                    j = 2 * half + jj
+                    if n == 0 and j == 0:
+                        for g in range(PASSES):
+                            quantize_x(0, g, 1, 2)
+                        accs[(0, 1)] = multiply(0, 0, 1)
+                    if n == 0 and j == 1:
+                        for g in range(PASSES):
+                            quantize_x(0, g, 2, 4)
+                        accs[(0, 2)] = multiply(0, 0, 2)
+                        accs[(0, 3)] = multiply(0, 0, 3)
+                        for j1 in range(GROUP):
+                            transpose_x(1, j1)
+                    if c == 0 and r + 1 < GROUPS and j == 3:
+                        quantize_x_group(r + 1)
+                    if c + 1 < SETS and r == GROUPS - 1 and j in (1, 2):
+                        quantize_w(c + 1, j - 1)
+                    if not last and j == 3:
+                        c1, r1 = steps[n + 1]
+                        for j1 in range(2):
+                            accs[(n + 1, j1)] = multiply(c1, r1, j1)
+                    if n > 0 and j == 0:
+                        for j1 in range(2, GROUP):
+                            accs[(n, j1)] = multiply(c, r, j1)
+                        if c == 0 and r + 1 < GROUPS:
+                            for j1 in range(GROUP):
+                                transpose_x(r + 1, j1)
+                        if c + 1 < SETS and r == GROUPS - 2:
+                            for h in range(HEADS):
+                                pack_w(c + 1, 0, h)
+                        if c + 1 < SETS and r == GROUPS - 1:
+                            for h in range(HEADS):
+                                pack_w(c + 1, 1, h)
+                    products(accs.pop((n, j)), r * GROUP + j, cos_part[:, jj], sin_part[:, jj])
+                engine = nc.vector if last and half == 1 else nc.gpsimd
+                engine.tensor_tensor(
+                    out=result[:, :, 2 * half : 2 * half + 2, :],
+                    in0=cos_part[:].rearrange("p j h c -> p h j c"),
+                    in1=sin_part[:].rearrange("p j h c -> p h j c"),
+                    op=op,
+                )
+                if last:
+                    s0 = r * GROUP + 2 * half
+                    nc.sync.dma_start(
+                        out=set_output(c)[:, :, s0 : s0 + 2, :], in_=result[:, :, 2 * half : 2 * half + 2, :]
+                    )
+            if not last:
+                nc.sync.dma_start(out=set_output(c)[:, :, r * GROUP : (r + 1) * GROUP, :], in_=result[:])

@@ -24,6 +24,8 @@ GROUPS = SLOTS // GROUP
 HEADS = 4
 SETS = 2 * H // HEADS
 PAIRS = QK // 2
+HALVES = 2
+UNITS = 2 * GROUPS * HALVES
 
 
 def tile_multiscaleretention_pa_kernel(tc, sequence, w_q, w_k, cos_half, sin_half, out_0, out_1):
@@ -41,50 +43,43 @@ def tile_multiscaleretention_pa_kernel(tc, sequence, w_q, w_k, cos_half, sin_hal
 
     with ExitStack() as ctx:
         keep = ctx.enter_context(tc.tile_pool(name="keep", bufs=1))
+        raw = ctx.enter_context(tc.tile_pool(name="raw", bufs=3))
         stage = ctx.enter_context(tc.tile_pool(name="stage", bufs=2))
         prod = ctx.enter_context(tc.tile_pool(name="prod", bufs=3))
-        res = ctx.enter_context(tc.tile_pool(name="res", bufs=3))
         psum_t = ctx.enter_context(tc.psum_pool(name="psum_t", bufs=2))
         psum_m = ctx.enter_context(tc.psum_pool(name="psum_m", bufs=6))
         ctx.enter_context(tc.manual_schedule())
 
-        x_raw = keep.tile([P, SLOTS, D], BF16, align_bytes=64)
-        w_raw = keep.tile([P, SETS, PASSES, HEADS, PACK, QK], BF16, align_bytes=64)
         cos_sb = keep.tile([P, SLOTS, PAIRS], BF16, align_bytes=64)
         sin_sb = keep.tile([P, SLOTS, PAIRS], BF16, align_bytes=64)
         sin_signed = keep.tile([P, SLOTS, PAIRS, 2], BF16, align_bytes=64)
+        cos_twice = keep.tile([P, SLOTS, PAIRS, 2], BF16, align_bytes=64)
+        tables = keep.tile([P, GROUPS, 2, GROUP * P], BF16, align_bytes=64)
         signs = keep.tile([P, 2], F32)
-        ident = keep.tile([P, P], F32)
+        ident = keep.tile([P, P], F32, align_bytes=64)
+        swap = keep.tile([P, P], F32, align_bytes=64)
+        ident_bf = keep.tile([P, P], BF16, align_bytes=64)
         x_codes = keep.tile([P, GROUPS, PASSES, GROUP * P], U32, align_bytes=64)
         x_scales = keep.tile([P, GROUPS, PASSES, GROUP * P], U8, align_bytes=64)
         w_codes = keep.tile([P, SETS, PASSES, HEADS * QK], U32, align_bytes=64)
         w_scales = keep.tile([P, SETS, PASSES, HEADS * QK], U8, align_bytes=64)
 
-        def load_x(s0, s1):
-            nc.sync.dma_start(out=x_raw[:, s0:s1, :], in_=x_hbm[:, s0:s1, :])
+        x_raw = {}
+        w_raw = {}
+
+        def load_x(r, j0, j1):
+            if j0 == 0:
+                x_raw[r] = raw.tile([P, GROUP, D], BF16, align_bytes=64, name="x_raw")
+            nc.sync.dma_start(out=x_raw[r][:, j0:j1, :], in_=x_hbm[:, r * GROUP + j0 : r * GROUP + j1, :])
 
         def load_w(c, g):
+            if g == 0:
+                w_raw[c] = raw.tile([P, PASSES, HEADS, PACK, QK], BF16, align_bytes=64, name="w_raw")
             rows = set_weights(c)[:, g * P * PACK : (g + 1) * P * PACK, :]
             nc.sync.dma_start(
-                out=w_raw[:, c, g].rearrange("p h t c -> p h (t c)"),
+                out=w_raw[c][:, g].rearrange("p h t c -> p h (t c)"),
                 in_=rows.rearrange("h (p t) c -> p h (t c)", t=PACK),
             )
-
-        load_x(0, 1)
-        nc.sync.dma_start(out=sin_sb[:], in_=sin_hbm)
-        load_w(0, 0)
-        load_w(0, 1)
-        nc.sync.dma_start(out=cos_sb[:], in_=cos_hbm)
-        load_x(1, GROUP)
-        for r in range(1, GROUPS):
-            load_x(r * GROUP, (r + 1) * GROUP)
-        for c in range(1, SETS):
-            for g in range(PASSES):
-                load_w(c, g)
-
-        make_identity(nc, ident[:])
-        nc.vector.memset(signs[:, 0:1], -1.0)
-        nc.vector.memset(signs[:, 1:2], 1.0)
 
         x_packed = {}
         w_packed = {}
@@ -92,7 +87,7 @@ def tile_multiscaleretention_pa_kernel(tc, sequence, w_q, w_k, cos_half, sin_hal
         def transpose_x(r, j):
             if j == 0:
                 x_packed[r] = stage.tile([P, PASSES, GROUP, P, PACK], BF16, align_bytes=64, name="x_packed")
-            words = x_raw[:, r * GROUP + j, :].bitcast(F32)
+            words = x_raw[r][:, j, :].bitcast(F32)
             bank = psum_t.tile([P, PASSES, 2, P], F32, name="bank_t")
             for g in range(PASSES):
                 for u in range(2):
@@ -103,14 +98,16 @@ def tile_multiscaleretention_pa_kernel(tc, sequence, w_q, w_k, cos_half, sin_hal
                 in_=bank[:].rearrange("p g u m -> p g m u"),
             )
 
-        def quantize_x(r, g, j0, j1):
-            nc.vector.quantize_mx(
-                out=x_codes[:, r, g, j0 * P : j1 * P].bitcast(E5M2),
-                scales=x_scales[:, r, g, j0 * P : j1 * P],
-                in_=x_packed[r][:, g, j0:j1].rearrange("p j m t -> p (j m t)"),
-            )
+        def quantize_x_half(r, half):
+            for g in range(PASSES):
+                cols = slice(2 * half * P, 2 * (half + 1) * P)
+                nc.vector.quantize_mx(
+                    out=x_codes[:, r, g, cols].bitcast(E5M2),
+                    scales=x_scales[:, r, g, cols],
+                    in_=x_packed[r][:, g, 2 * half : 2 * half + 2].rearrange("p j m t -> p (j m t)"),
+                )
 
-        def quantize_x_group(r):
+        def quantize_x(r):
             nc.vector.quantize_mx(
                 out=x_codes[:, r].rearrange("p g m -> p (g m)").bitcast(E5M2),
                 scales=x_scales[:, r].rearrange("p g m -> p (g m)"),
@@ -121,11 +118,20 @@ def tile_multiscaleretention_pa_kernel(tc, sequence, w_q, w_k, cos_half, sin_hal
             if c not in w_packed:
                 w_packed[c] = stage.tile([P, PASSES, HEADS, QK, PACK], BF16, align_bytes=64, name="w_packed")
             dst = w_packed[c][:, g, h].rearrange("p (n i) t -> p n t i", i=4)
-            src = w_raw[:, c, g, h].rearrange("p t (n i) -> p n t i", i=4)
+            src = w_raw[c][:, g, h].rearrange("p t (n i) -> p n t i", i=4)
             if on_vector:
                 nc.vector.tensor_copy(out=dst, in_=src)
             else:
                 nc.scalar.copy(out=dst, in_=src)
+
+        def pack_w_set(c):
+            for g in range(PASSES):
+                for h in range(HEADS):
+                    pack_w(c, g, h)
+
+        def transpose_x_group(r):
+            for j in range(GROUP):
+                transpose_x(r, j)
 
         def quantize_w(c, g):
             nc.vector.quantize_mx(
@@ -134,114 +140,263 @@ def tile_multiscaleretention_pa_kernel(tc, sequence, w_q, w_k, cos_half, sin_hal
                 in_=w_packed[c][:, g].rearrange("p h n t -> p (h n t)"),
             )
 
-        def multiply(c, r, j):
-            acc = psum_m.tile([P, HEADS * QK], F32, name="acc")
-            for g in range(PASSES):
-                nc.tensor.matmul_mx(
-                    out=acc[:],
-                    lhsT=x_codes[:, r, g, j * P : (j + 1) * P].bitcast(E5M2),
-                    lhsT_scale=x_scales[:, r, g, j * P : (j + 1) * P],
-                    rhs=w_codes[:, c, g].bitcast(E4M3),
-                    rhs_scale=w_scales[:, c, g],
-                    start=(g == 0),
-                    stop=(g == PASSES - 1),
-                )
-            return acc
+        def quantize_w_set(c):
+            nc.vector.quantize_mx(
+                out=w_codes[:, c].rearrange("p g m -> p (g m)").bitcast(E4M3),
+                scales=w_scales[:, c].rearrange("p g m -> p (g m)"),
+                in_=w_packed[c][:].rearrange("p g h n t -> p (g h n t)"),
+            )
+
+        def widen_sin(engine, r0, r1):
+            slots = slice(r0 * GROUP, r1 * GROUP)
+            shape = [P, (r1 - r0) * GROUP * PAIRS, 2]
+            engine.tensor_tensor(
+                out=sin_signed[:, slots].rearrange("p s i e -> p (s i) e"),
+                in0=sin_sb[:, slots].rearrange("p s i -> p (s i)").unsqueeze(2).to_broadcast(shape),
+                in1=signs[:].unsqueeze(1).to_broadcast(shape),
+                op=ALU.mult,
+            )
+
+        def widen_cos(r):
+            slots = slice(r * GROUP, (r + 1) * GROUP)
+            nc.scalar.copy(
+                out=cos_twice[:, slots].rearrange("p s i e -> p (s i) e"),
+                in_=cos_sb[:, slots].rearrange("p s i -> p (s i)").unsqueeze(2).to_broadcast([P, GROUP * PAIRS, 2]),
+            )
+
+        def transpose_tables(r):
+            bank = psum_t.tile([P, PASSES, 2, P], F32, name="bank_t")
+            flat = bank[:].rearrange("p g u m -> p (g u m)").bitcast(BF16)
+            for a, table in enumerate((cos_twice, sin_signed)):
+                for j in range(GROUP):
+                    col = (a * GROUP + j) * P
+                    nc.tensor.transpose(
+                        flat[:, col : col + P], table[:, r * GROUP + j].rearrange("p i e -> p (i e)"), ident_bf[:]
+                    )
+            nc.scalar.copy(out=tables[:, r].rearrange("p a m -> p (a m)"), in_=flat)
+
+        def unit(n):
+            return n // (GROUPS * HALVES), n % (GROUPS * HALVES) // HALVES, n % HALVES
+
+        def mx_pair(stationary, moving, fmt_s, fmt_m):
+            banks = []
+            for (s_codes, s_scales), (m_codes, m_scales) in zip(stationary, moving):
+                acc = psum_m.tile([P, 4 * P], F32, name="acc")
+                for g in range(PASSES):
+                    nc.tensor.matmul_mx(
+                        out=acc[:],
+                        lhsT=s_codes[:, g].bitcast(fmt_s),
+                        lhsT_scale=s_scales[:, g],
+                        rhs=m_codes[:, g].bitcast(fmt_m),
+                        rhs_scale=m_scales[:, g],
+                        start=(g == 0),
+                        stop=(g == PASSES - 1),
+                    )
+                banks.append(acc)
+            return banks
+
+        q_banks = {}
+        k_banks = {}
+        q_result = {}
+        k_parts = {}
+
+        def multiply_q(n):
+            c, r, half = unit(n)
+            cols = [slice((2 * half + a) * P, (2 * half + a + 1) * P) for a in range(2)]
+            q_banks[n] = mx_pair(
+                [(x_codes[:, r, :, s], x_scales[:, r, :, s]) for s in cols],
+                [(w_codes[:, c], w_scales[:, c])] * 2,
+                E5M2,
+                E4M3,
+            )
+
+        def multiply_k(n):
+            c, r, half = unit(n)
+            cols = [slice((2 * half + a) * QK, (2 * half + a + 1) * QK) for a in range(2)]
+            k_banks[n] = mx_pair(
+                [(w_codes[:, 2 + c, :, s], w_scales[:, 2 + c, :, s]) for s in cols],
+                [(x_codes[:, r], x_scales[:, r])] * 2,
+                E4M3,
+                E5M2,
+            )
 
         shape4 = [P, HEADS, PAIRS, 2]
 
-        def products(acc, s, cos_part, sin_part):
-            pairs = acc[:].rearrange("p (h i e) -> p h i e", h=HEADS, e=2)
-            nc.vector.tensor_tensor(
-                out=cos_part.rearrange("p h (i e) -> p h i e", e=2),
-                in0=pairs,
-                in1=cos_sb[:, s, :].unsqueeze(1).unsqueeze(3).to_broadcast(shape4),
-                op=ALU.mult,
+        def rotate_q(n):
+            c, r, half = unit(n)
+            if half == 0:
+                q_result[n // 2] = prod.tile([P, HEADS, GROUP, QK], F32, name="q_result")
+            result = q_result[n // 2]
+            cos_part = prod.tile([P, 2, HEADS, QK], F32, name="q_cos_part")
+            sin_part = prod.tile([P, 2, HEADS, QK], F32, name="q_sin_part")
+            for a in (1, 0):
+                s = r * GROUP + 2 * half + a
+                pairs = q_banks[n][a][:].rearrange("p (h i e) -> p h i e", h=HEADS, e=2)
+                nc.vector.tensor_tensor(
+                    out=cos_part[:, a].rearrange("p h (i e) -> p h i e", e=2),
+                    in0=pairs,
+                    in1=cos_sb[:, s, :].unsqueeze(1).unsqueeze(3).to_broadcast(shape4),
+                    op=ALU.mult,
+                )
+                nc.vector.tensor_tensor(
+                    out=sin_part[:, a].rearrange("p h (i e) -> p h i e", e=2),
+                    in0=pairs[:, :, :, ::-1],
+                    in1=sin_signed[:, s].unsqueeze(1).to_broadcast(shape4),
+                    op=ALU.mult,
+                )
+            nc.gpsimd.tensor_tensor(
+                out=result[:, :, 2 * half : 2 * half + 2, :],
+                in0=cos_part[:].rearrange("p j h c -> p h j c"),
+                in1=sin_part[:].rearrange("p j h c -> p h j c"),
+                op=ALU.add,
             )
-            nc.vector.tensor_tensor(
-                out=sin_part.rearrange("p h (i e) -> p h i e", e=2),
-                in0=pairs[:, :, :, ::-1],
-                in1=sin_signed[:, s].unsqueeze(1).to_broadcast(shape4),
-                op=ALU.mult,
-            )
+            if n >= UNITS - 2:
+                s0 = r * GROUP + 2 * half
+                nc.sync.dma_start(out=set_output(c)[:, :, s0 : s0 + 2, :], in_=result[:, :, 2 * half : 2 * half + 2, :])
+            elif half == 1:
+                nc.sync.dma_start(out=set_output(c)[:, :, r * GROUP : (r + 1) * GROUP, :], in_=result[:])
 
-        transpose_x(0, 0)
-        nc.vector.tensor_tensor(
-            out=sin_signed[:].rearrange("p s i e -> p (s i) e"),
-            in0=sin_sb[:].rearrange("p s i -> p (s i)").unsqueeze(2).to_broadcast([P, SLOTS * PAIRS, 2]),
-            in1=signs[:].unsqueeze(1).to_broadcast([P, SLOTS * PAIRS, 2]),
-            op=ALU.mult,
+        def products_k(n):
+            c, r, half = unit(n)
+            cos_part = prod.tile([P, 2, GROUP * P], F32, name="k_cos_part")
+            sin_part = prod.tile([P, 2, GROUP * P], F32, name="k_sin_part")
+            k_parts[n] = (cos_part, sin_part)
+            shared = gpsimd_helps(n)
+            if shared:
+                k_sb = stage.tile([P, 2, GROUP * P], F32, name="k_sb")
+            for a in (0, 1) if n == UNITS - 1 else (1, 0):
+                bank = k_banks[n][a]
+                nc.vector.tensor_tensor(out=sin_part[:, a], in0=bank[:], in1=tables[:, r, 1], op=ALU.mult)
+                if shared:
+                    nc.scalar.copy(out=k_sb[:, a], in_=bank[:])
+                else:
+                    nc.vector.tensor_tensor(out=cos_part[:, a], in0=bank[:], in1=tables[:, r, 0], op=ALU.mult)
+            if shared:
+                nc.gpsimd.tensor_tensor(
+                    out=cos_part[:],
+                    in0=k_sb[:],
+                    in1=tables[:, r, 0].unsqueeze(1).to_broadcast([P, 2, GROUP * P]),
+                    op=ALU.mult,
+                )
+
+        def finish_k(n):
+            c, r, half = unit(n)
+            cos_part, sin_part = k_parts[n]
+            result = prod.tile([P, 2, GROUP * QK], F32, name="k_result")
+            heads = set_output(2 + c)[:, 2 * half : 2 * half + 2, r * GROUP : (r + 1) * GROUP, :]
+            heads = heads.rearrange("p h s c -> p h (s c)")
+            for a in range(2):
+                bank = psum_t.tile([P, PASSES, 2, P], F32, name="bank_t")
+                flat = bank[:].rearrange("p g u m -> p (g u m)")
+                for j in range(GROUP):
+                    cols = slice(j * P, (j + 1) * P)
+                    nc.tensor.matmul(
+                        flat[:, cols], lhsT=sin_part[:, a, cols], rhs=swap[:], start=True, stop=False, is_transpose=True
+                    )
+                    nc.tensor.matmul(
+                        flat[:, cols], lhsT=cos_part[:, a, cols], rhs=ident[:], start=False, stop=True, is_transpose=True
+                    )
+                nc.scalar.copy(out=result[:, a], in_=flat)
+                if n == UNITS - 1:
+                    nc.sync.dma_start(out=heads[:, a], in_=result[:, a])
+            if n < UNITS - 1:
+                nc.sync.dma_start(out=heads, in_=result[:])
+
+        def gpsimd_helps(n):
+            return n % 2 == 0 and 4 <= n < 14
+
+        nc.sync.dma_start(out=sin_sb[:, :GROUP], in_=sin_hbm[:, :GROUP])
+        nc.sync.dma_start(out=cos_sb[:, :GROUP], in_=cos_hbm[:, :GROUP])
+        load_w(0, 0)
+        load_x(0, 0, 2)
+        load_w(0, 1)
+        load_x(0, 2, GROUP)
+        load_w(2, 0)
+        load_w(2, 1)
+        nc.sync.dma_start(out=sin_sb[:, GROUP:], in_=sin_hbm[:, GROUP:])
+        nc.sync.dma_start(out=cos_sb[:, GROUP:], in_=cos_hbm[:, GROUP:])
+        load_x(1, 0, GROUP)
+        load_x(2, 0, GROUP)
+        load_w(1, 0)
+        load_w(1, 1)
+
+        make_identity(nc, ident[:])
+        make_identity(nc, ident_bf[:])
+        nc.vector.memset(signs[:, 0:1], -1.0)
+        nc.vector.memset(signs[:, 1:2], 1.0)
+        nc.vector.tensor_copy(
+            out=swap[:].rearrange("p (i e) -> p i e", e=2), in_=ident[:].rearrange("p (i e) -> p i e", e=2)[:, :, ::-1]
         )
-        pack_w(0, 0, 0)
-        for h in range(1, HEADS):
-            pack_w(0, 0, h, on_vector=True)
-        for g in range(PASSES):
-            quantize_x(0, g, 0, 1)
-        quantize_w(0, 0)
-        pack_w(0, 1, 0)
-        pack_w(0, 1, 1)
-        pack_w(0, 1, 2, on_vector=True)
-        pack_w(0, 1, 3, on_vector=True)
+        widen_sin(nc.vector, 0, 1)
+        widen_cos(0)
+        transpose_tables(0)
+        transpose_x(0, 0)
         transpose_x(0, 1)
-        quantize_w(0, 1)
-
-        steps = [(c, r) for c in range(SETS) for r in range(GROUPS)]
-        accs = {(0, 0): multiply(0, 0, 0)}
+        for g in range(PASSES):
+            for h in range(HEADS):
+                pack_w(0, g, h, on_vector=True)
+            quantize_w(0, g)
+        quantize_x_half(0, 0)
         transpose_x(0, 2)
         transpose_x(0, 3)
+        multiply_q(0)
+        quantize_x_half(0, 1)
+        load_x(3, 0, GROUP)
+        load_w(3, 0)
+        load_w(3, 1)
+        pack_w_set(2)
 
-        for n, (c, r) in enumerate(steps):
-            last = n == len(steps) - 1
-            result = res.tile([P, HEADS, GROUP, QK], F32, name="result")
-            op = ALU.add if c < SETS // 2 else ALU.subtract
-            for half in range(2):
-                cos_part = prod.tile([P, 2, HEADS, QK], F32, name="cos_part")
-                sin_part = prod.tile([P, 2, HEADS, QK], F32, name="sin_part")
-                for jj in range(2):
-                    j = 2 * half + jj
-                    if n == 0 and j == 0:
-                        for g in range(PASSES):
-                            quantize_x(0, g, 1, 2)
-                        accs[(0, 1)] = multiply(0, 0, 1)
-                    if n == 0 and j == 1:
-                        for g in range(PASSES):
-                            quantize_x(0, g, 2, 4)
-                        accs[(0, 2)] = multiply(0, 0, 2)
-                        accs[(0, 3)] = multiply(0, 0, 3)
-                        for j1 in range(GROUP):
-                            transpose_x(1, j1)
-                    if c == 0 and r + 1 < GROUPS and j == 3:
-                        quantize_x_group(r + 1)
-                    if c + 1 < SETS and r == GROUPS - 1 and j in (1, 2):
-                        quantize_w(c + 1, j - 1)
-                    if not last and j == 3:
-                        c1, r1 = steps[n + 1]
-                        for j1 in range(2):
-                            accs[(n + 1, j1)] = multiply(c1, r1, j1)
-                    if n > 0 and j == 0:
-                        for j1 in range(2, GROUP):
-                            accs[(n, j1)] = multiply(c, r, j1)
-                        if c == 0 and r + 1 < GROUPS:
-                            for j1 in range(GROUP):
-                                transpose_x(r + 1, j1)
-                        if c + 1 < SETS and r == GROUPS - 2:
-                            for h in range(HEADS):
-                                pack_w(c + 1, 0, h)
-                        if c + 1 < SETS and r == GROUPS - 1:
-                            for h in range(HEADS):
-                                pack_w(c + 1, 1, h)
-                    products(accs.pop((n, j)), r * GROUP + j, cos_part[:, jj], sin_part[:, jj])
-                engine = nc.vector if last and half == 1 else nc.gpsimd
-                engine.tensor_tensor(
-                    out=result[:, :, 2 * half : 2 * half + 2, :],
-                    in0=cos_part[:].rearrange("p j h c -> p h j c"),
-                    in1=sin_part[:].rearrange("p j h c -> p h j c"),
-                    op=op,
-                )
-                if last:
-                    s0 = r * GROUP + 2 * half
-                    nc.sync.dma_start(
-                        out=set_output(c)[:, :, s0 : s0 + 2, :], in_=result[:, :, 2 * half : 2 * half + 2, :]
-                    )
+        steps = 2 * GROUPS
+        for s in range(steps):
+            n = 2 * s
+            last = s == steps - 1
+            multiply_q(n + 1)
+            if s > 0:
+                finish_k(n - 1)
+            if s == 0:
+                transpose_x_group(1)
+            if s == 1:
+                transpose_x_group(3)
+            for c, g in {1: [(1, 1)], 2: [(3, 0)], 3: [(3, 1)]}.get(s, []):
+                for h in range(HEADS):
+                    pack_w(c, g, h)
+            rotate_q(n)
+            if s == 0:
+                quantize_w(2, 0)
+            if s == 1:
+                widen_sin(nc.gpsimd, 2, GROUPS)
+            if s == 2:
+                quantize_x(3)
+            if s in (3, 4):
+                quantize_w_set(2 * s - 5)
+            if s > 0:
+                multiply_k(n)
+                multiply_k(n + 1)
+            rotate_q(n + 1)
+            if s == 0:
+                quantize_w(2, 1)
+                widen_sin(nc.gpsimd, 1, 2)
+                multiply_k(n)
+                multiply_k(n + 1)
+                for r in range(1, GROUPS):
+                    widen_cos(r)
+                transpose_x_group(2)
+                transpose_tables(1)
+                for h in range(HEADS):
+                    pack_w(1, 0, h)
+            if last:
+                finish_k(n - 2)
+            products_k(n)
+            if 0 < s < steps - 1:
+                finish_k(n - 2)
+            if s == 0:
+                quantize_x(1)
             if not last:
-                nc.sync.dma_start(out=set_output(c)[:, :, r * GROUP : (r + 1) * GROUP, :], in_=result[:])
+                multiply_q(n + 2)
+            if s in (1, 2):
+                transpose_tables(s + 1)
+            products_k(n + 1)
+            if s == 0:
+                quantize_x(2)
+        finish_k(UNITS - 2)
+        finish_k(UNITS - 1)

@@ -26,6 +26,7 @@ SETS = 2 * H // HEADS
 PAIRS = QK // 2
 HALVES = 2
 UNITS = 2 * GROUPS * HALVES
+TOKEN_K = 2
 
 
 def tile_multiscaleretention_pa_kernel(tc, sequence, w_q, w_k, cos_half, sin_half, out_0, out_1):
@@ -46,6 +47,7 @@ def tile_multiscaleretention_pa_kernel(tc, sequence, w_q, w_k, cos_half, sin_hal
         raw = ctx.enter_context(tc.tile_pool(name="raw", bufs=3))
         stage = ctx.enter_context(tc.tile_pool(name="stage", bufs=2))
         prod = ctx.enter_context(tc.tile_pool(name="prod", bufs=3))
+        parts = ctx.enter_context(tc.tile_pool(name="parts", bufs=4))
         psum_t = ctx.enter_context(tc.psum_pool(name="psum_t", bufs=2))
         psum_m = ctx.enter_context(tc.psum_pool(name="psum_m", bufs=6))
         ctx.enter_context(tc.manual_schedule())
@@ -124,11 +126,6 @@ def tile_multiscaleretention_pa_kernel(tc, sequence, w_q, w_k, cos_half, sin_hal
             else:
                 nc.scalar.copy(out=dst, in_=src)
 
-        def pack_w_set(c):
-            for g in range(PASSES):
-                for h in range(HEADS):
-                    pack_w(c, g, h)
-
         def transpose_x_group(r):
             for j in range(GROUP):
                 transpose_x(r, j)
@@ -179,10 +176,9 @@ def tile_multiscaleretention_pa_kernel(tc, sequence, w_q, w_k, cos_half, sin_hal
             return n // (GROUPS * HALVES), n % (GROUPS * HALVES) // HALVES, n % HALVES
 
         def mx_pair(stationary, moving, fmt_s, fmt_m):
-            banks = []
-            for (s_codes, s_scales), (m_codes, m_scales) in zip(stationary, moving):
-                acc = psum_m.tile([P, 4 * P], F32, name="acc")
-                for g in range(PASSES):
+            banks = [psum_m.tile([P, 4 * P], F32, name="acc") for a in range(2)]
+            for g in range(PASSES):
+                for acc, (s_codes, s_scales), (m_codes, m_scales) in zip(banks, stationary, moving):
                     nc.tensor.matmul_mx(
                         out=acc[:],
                         lhsT=s_codes[:, g].bitcast(fmt_s),
@@ -192,7 +188,6 @@ def tile_multiscaleretention_pa_kernel(tc, sequence, w_q, w_k, cos_half, sin_hal
                         start=(g == 0),
                         stop=(g == PASSES - 1),
                     )
-                banks.append(acc)
             return banks
 
         q_banks = {}
@@ -200,10 +195,11 @@ def tile_multiscaleretention_pa_kernel(tc, sequence, w_q, w_k, cos_half, sin_hal
         q_result = {}
         k_parts = {}
 
-        def multiply_q(n):
+        def multiply_q(n, out=0):
             c, r, half = unit(n)
+            c += 2 * out
             cols = [slice((2 * half + a) * P, (2 * half + a + 1) * P) for a in range(2)]
-            q_banks[n] = mx_pair(
+            q_banks[n, out] = mx_pair(
                 [(x_codes[:, r, :, s], x_scales[:, r, :, s]) for s in cols],
                 [(w_codes[:, c], w_scales[:, c])] * 2,
                 E5M2,
@@ -211,6 +207,8 @@ def tile_multiscaleretention_pa_kernel(tc, sequence, w_q, w_k, cos_half, sin_hal
             )
 
         def multiply_k(n):
+            if n < TOKEN_K:
+                return multiply_q(n, 1)
             c, r, half = unit(n)
             cols = [slice((2 * half + a) * QK, (2 * half + a + 1) * QK) for a in range(2)]
             k_banks[n] = mx_pair(
@@ -222,16 +220,17 @@ def tile_multiscaleretention_pa_kernel(tc, sequence, w_q, w_k, cos_half, sin_hal
 
         shape4 = [P, HEADS, PAIRS, 2]
 
-        def rotate_q(n):
+        def rotate_q(n, out=0):
             c, r, half = unit(n)
+            c += 2 * out
             if half == 0:
-                q_result[n // 2] = prod.tile([P, HEADS, GROUP, QK], F32, name="q_result")
-            result = q_result[n // 2]
+                q_result[n // 2, out] = prod.tile([P, HEADS, GROUP, QK], F32, name="q_result")
+            result = q_result[n // 2, out]
             cos_part = prod.tile([P, 2, HEADS, QK], F32, name="q_cos_part")
             sin_part = prod.tile([P, 2, HEADS, QK], F32, name="q_sin_part")
             for a in (1, 0):
                 s = r * GROUP + 2 * half + a
-                pairs = q_banks[n][a][:].rearrange("p (h i e) -> p h i e", h=HEADS, e=2)
+                pairs = q_banks[n, out][a][:].rearrange("p (h i e) -> p h i e", h=HEADS, e=2)
                 nc.vector.tensor_tensor(
                     out=cos_part[:, a].rearrange("p h (i e) -> p h i e", e=2),
                     in0=pairs,
@@ -248,7 +247,7 @@ def tile_multiscaleretention_pa_kernel(tc, sequence, w_q, w_k, cos_half, sin_hal
                 out=result[:, :, 2 * half : 2 * half + 2, :],
                 in0=cos_part[:].rearrange("p j h c -> p h j c"),
                 in1=sin_part[:].rearrange("p j h c -> p h j c"),
-                op=ALU.add,
+                op=ALU.subtract if out else ALU.add,
             )
             if n >= UNITS - 2:
                 s0 = r * GROUP + 2 * half
@@ -257,29 +256,33 @@ def tile_multiscaleretention_pa_kernel(tc, sequence, w_q, w_k, cos_half, sin_hal
                 nc.sync.dma_start(out=set_output(c)[:, :, r * GROUP : (r + 1) * GROUP, :], in_=result[:])
 
         def products_k(n):
+            if n < TOKEN_K:
+                return rotate_q(n, 1)
             c, r, half = unit(n)
-            cos_part = prod.tile([P, 2, GROUP * P], F32, name="k_cos_part")
-            sin_part = prod.tile([P, 2, GROUP * P], F32, name="k_sin_part")
+            cos_part = parts.tile([P, 2, GROUP * P], F32, name="k_cos_part")
+            sin_part = parts.tile([P, 2, GROUP * P], F32, name="k_sin_part")
             k_parts[n] = (cos_part, sin_part)
-            shared = gpsimd_helps(n)
-            if shared:
-                k_sb = stage.tile([P, 2, GROUP * P], F32, name="k_sb")
-            for a in (0, 1) if n == UNITS - 1 else (1, 0):
+            order = (0, 1) if n == UNITS - 1 else (1, 0)
+            shared = gpsimd_banks(n)
+            for a in order:
                 bank = k_banks[n][a]
-                nc.vector.tensor_tensor(out=sin_part[:, a], in0=bank[:], in1=tables[:, r, 1], op=ALU.mult)
-                if shared:
-                    nc.scalar.copy(out=k_sb[:, a], in_=bank[:])
+                if a >= 2 - shared:
+                    nc.vector.tensor_tensor(out=sin_part[:, a], in0=bank[:], in1=tables[:, r, 1], op=ALU.mult)
+                    nc.scalar.copy(out=cos_part[:, a], in_=bank[:])
                 else:
                     nc.vector.tensor_tensor(out=cos_part[:, a], in0=bank[:], in1=tables[:, r, 0], op=ALU.mult)
+                    nc.vector.tensor_tensor(out=sin_part[:, a], in0=bank[:], in1=tables[:, r, 1], op=ALU.mult)
             if shared:
                 nc.gpsimd.tensor_tensor(
-                    out=cos_part[:],
-                    in0=k_sb[:],
-                    in1=tables[:, r, 0].unsqueeze(1).to_broadcast([P, 2, GROUP * P]),
+                    out=cos_part[:, 2 - shared :],
+                    in0=cos_part[:, 2 - shared :],
+                    in1=tables[:, r, 0].unsqueeze(1).to_broadcast([P, shared, GROUP * P]),
                     op=ALU.mult,
                 )
 
         def finish_k(n):
+            if n < TOKEN_K:
+                return
             c, r, half = unit(n)
             cos_part, sin_part = k_parts[n]
             result = prod.tile([P, 2, GROUP * QK], F32, name="k_result")
@@ -302,20 +305,21 @@ def tile_multiscaleretention_pa_kernel(tc, sequence, w_q, w_k, cos_half, sin_hal
             if n < UNITS - 1:
                 nc.sync.dma_start(out=heads, in_=result[:])
 
-        def gpsimd_helps(n):
-            return n % 2 == 0 and 4 <= n < 14
+        def gpsimd_banks(n):
+            return 2 if n % 2 == 0 and 4 <= n < 14 else 0
 
-        nc.sync.dma_start(out=sin_sb[:, :GROUP], in_=sin_hbm[:, :GROUP])
-        nc.sync.dma_start(out=cos_sb[:, :GROUP], in_=cos_hbm[:, :GROUP])
+        nc.sync.dma_start(out=sin_sb[:, : 2 * GROUP], in_=sin_hbm[:, : 2 * GROUP])
         load_w(0, 0)
         load_x(0, 0, 2)
         load_w(0, 1)
+        nc.sync.dma_start(out=cos_sb[:, :GROUP], in_=cos_hbm[:, :GROUP])
         load_x(0, 2, GROUP)
         load_w(2, 0)
         load_w(2, 1)
-        nc.sync.dma_start(out=sin_sb[:, GROUP:], in_=sin_hbm[:, GROUP:])
+        load_x(1, 0, 2)
+        load_x(1, 2, GROUP)
+        nc.sync.dma_start(out=sin_sb[:, 2 * GROUP :], in_=sin_hbm[:, 2 * GROUP :])
         nc.sync.dma_start(out=cos_sb[:, GROUP:], in_=cos_hbm[:, GROUP:])
-        load_x(1, 0, GROUP)
         load_x(2, 0, GROUP)
         load_w(1, 0)
         load_w(1, 1)
@@ -327,24 +331,27 @@ def tile_multiscaleretention_pa_kernel(tc, sequence, w_q, w_k, cos_half, sin_hal
         nc.vector.tensor_copy(
             out=swap[:].rearrange("p (i e) -> p i e", e=2), in_=ident[:].rearrange("p (i e) -> p i e", e=2)[:, :, ::-1]
         )
-        widen_sin(nc.vector, 0, 1)
-        widen_cos(0)
-        transpose_tables(0)
+        widen_sin(nc.vector, 0, 2)
         transpose_x(0, 0)
         transpose_x(0, 1)
-        for g in range(PASSES):
-            for h in range(HEADS):
-                pack_w(0, g, h, on_vector=True)
-            quantize_w(0, g)
+        for h in range(HEADS):
+            pack_w(0, 0, h, on_vector=True)
+        quantize_w(0, 0)
+        for h in range(HEADS):
+            pack_w(0, 1, h, on_vector=h >= 1)
         quantize_x_half(0, 0)
+        quantize_w(0, 1)
         transpose_x(0, 2)
         transpose_x(0, 3)
         multiply_q(0)
+        for h in range(4):
+            pack_w(2, 0, h, on_vector=True)
         quantize_x_half(0, 1)
         load_x(3, 0, GROUP)
         load_w(3, 0)
         load_w(3, 1)
-        pack_w_set(2)
+        for g, h in [(g, h) for g in range(PASSES) for h in range(HEADS)][4:]:
+            pack_w(2, g, h)
 
         steps = 2 * GROUPS
         for s in range(steps):
@@ -355,35 +362,31 @@ def tile_multiscaleretention_pa_kernel(tc, sequence, w_q, w_k, cos_half, sin_hal
                 finish_k(n - 1)
             if s == 0:
                 transpose_x_group(1)
-            if s == 1:
-                transpose_x_group(3)
             for c, g in {1: [(1, 1)], 2: [(3, 0)], 3: [(3, 1)]}.get(s, []):
                 for h in range(HEADS):
                     pack_w(c, g, h)
             rotate_q(n)
             if s == 0:
-                quantize_w(2, 0)
+                quantize_w_set(2)
+            if s in (1, 2):
+                quantize_x(s + 1)
             if s == 1:
                 widen_sin(nc.gpsimd, 2, GROUPS)
-            if s == 2:
-                quantize_x(3)
             if s in (3, 4):
                 quantize_w_set(2 * s - 5)
             if s > 0:
                 multiply_k(n)
                 multiply_k(n + 1)
+            if s == 1:
+                transpose_x(3, 0)
+                transpose_x(3, 1)
             rotate_q(n + 1)
             if s == 0:
-                quantize_w(2, 1)
-                widen_sin(nc.gpsimd, 1, 2)
                 multiply_k(n)
                 multiply_k(n + 1)
-                for r in range(1, GROUPS):
-                    widen_cos(r)
-                transpose_x_group(2)
-                transpose_tables(1)
-                for h in range(HEADS):
-                    pack_w(1, 0, h)
+                widen_cos(1)
+                transpose_x(2, 0)
+                transpose_x(2, 1)
             if last:
                 finish_k(n - 2)
             products_k(n)
@@ -393,10 +396,22 @@ def tile_multiscaleretention_pa_kernel(tc, sequence, w_q, w_k, cos_half, sin_hal
                 quantize_x(1)
             if not last:
                 multiply_q(n + 2)
+            if s == 0:
+                transpose_x(2, 2)
+                transpose_x(2, 3)
+                transpose_tables(1)
+                widen_cos(2)
+                for h in range(HEADS):
+                    pack_w(1, 0, h)
+            if s == 1:
+                transpose_x(3, 2)
+                transpose_x(3, 3)
             if s in (1, 2):
                 transpose_tables(s + 1)
+            if s in (1, 2):
+                widen_cos((s + 2) % GROUPS)
+            if s == 3:
+                transpose_tables(0)
             products_k(n + 1)
-            if s == 0:
-                quantize_x(2)
         finish_k(UNITS - 2)
         finish_k(UNITS - 1)

from contextlib import ExitStack

import concourse.mybir as mybir
from concourse.masks import make_identity

B, L, D, H, QK = 4, 512, 1024, 8, 128
T = B * L
FLOPS = 2 * T * D * 2 * H * QK

F32 = mybir.dt.float32
BF16 = mybir.dt.bfloat16
U32 = mybir.dt.uint32
U8 = mybir.dt.uint8
E5M2 = mybir.dt.float8_e5m2_x4
E4M3 = mybir.dt.float8_e4m3fn_x4
ALU = mybir.AluOpType

P = 128
PACK = 4
PASSES = D // (P * PACK)
SLOTS = T // P
GROUP = 4
GROUPS = SLOTS // GROUP
HEADS = 4
SETS = 2 * H // HEADS
PAIRS = QK // 2
HALVES = 2
UNITS = 2 * GROUPS * HALVES
TOKEN_K = 2


def tile_multiscaleretention_pa_kernel(tc, sequence, w_q, w_k, cos_half, sin_half, out_0, out_1):
    nc = tc.nc
    x_hbm = sequence.rearrange("b l d -> (b l) d").rearrange("(p s) d -> p s d", p=P)
    cos_hbm = cos_half.rearrange("b l i -> (b l) i").rearrange("(p s) i -> p s i", p=P)
    sin_hbm = sin_half.rearrange("b l i -> (b l) i").rearrange("(p s) i -> p s i", p=P)

    def set_weights(c):
        return (w_q, w_k)[c // 2][(c % 2) * HEADS : (c % 2 + 1) * HEADS]

    def set_output(c):
        heads = (out_0, out_1)[c // 2][(c % 2) * HEADS : (c % 2 + 1) * HEADS]
        return heads.rearrange("h b l c -> h (b l) c").rearrange("h (p s) c -> p h s c", p=P)

    with ExitStack() as ctx:
        keep = ctx.enter_context(tc.tile_pool(name="keep", bufs=1))
        raw = ctx.enter_context(tc.tile_pool(name="raw", bufs=3))
        stage = ctx.enter_context(tc.tile_pool(name="stage", bufs=2))
        prod = ctx.enter_context(tc.tile_pool(name="prod", bufs=3))
        parts = ctx.enter_context(tc.tile_pool(name="parts", bufs=4))
        psum_t = ctx.enter_context(tc.psum_pool(name="psum_t", bufs=2))
        psum_m = ctx.enter_context(tc.psum_pool(name="psum_m", bufs=6))
        ctx.enter_context(tc.manual_schedule())

        cos_sb = keep.tile([P, SLOTS, PAIRS], BF16, align_bytes=64)
        sin_sb = keep.tile([P, SLOTS, PAIRS], BF16, align_bytes=64)
        sin_signed = keep.tile([P, SLOTS, PAIRS, 2], BF16, align_bytes=64)
        cos_twice = keep.tile([P, SLOTS, PAIRS, 2], BF16, align_bytes=64)
        tables = keep.tile([P, GROUPS, 2, GROUP * P], BF16, align_bytes=64)
        signs = keep.tile([P, 2], F32)
        ident = keep.tile([P, P], F32, align_bytes=64)
        swap = keep.tile([P, P], F32, align_bytes=64)
        ident_bf = keep.tile([P, P], BF16, align_bytes=64)
        x_codes = keep.tile([P, GROUPS, PASSES, GROUP * P], U32, align_bytes=64)
        x_scales = keep.tile([P, GROUPS, PASSES, GROUP * P], U8, align_bytes=64)
        w_codes = keep.tile([P, SETS, PASSES, HEADS * QK], U32, align_bytes=64)
        w_scales = keep.tile([P, SETS, PASSES, HEADS * QK], U8, align_bytes=64)

        x_raw = {}
        w_raw = {}

        def load_x(r, j0, j1):
            if j0 == 0:
                x_raw[r] = raw.tile([P, GROUP, D], BF16, align_bytes=64, name="x_raw")
            nc.sync.dma_start(out=x_raw[r][:, j0:j1, :], in_=x_hbm[:, r * GROUP + j0 : r * GROUP + j1, :])

        def load_w(c, g):
            if g == 0:
                w_raw[c] = raw.tile([P, PASSES, HEADS, PACK, QK], BF16, align_bytes=64, name="w_raw")
            rows = set_weights(c)[:, g * P * PACK : (g + 1) * P * PACK, :]
            nc.sync.dma_start(
                out=w_raw[c][:, g].rearrange("p h t c -> p h (t c)"),
                in_=rows.rearrange("h (p t) c -> p h (t c)", t=PACK),
            )

        x_packed = {}
        w_packed = {}

        def transpose_x(r, j):
            if j == 0:
                x_packed[r] = stage.tile([P, PASSES, GROUP, P, PACK], BF16, align_bytes=64, name="x_packed")
            words = x_raw[r][:, j, :].bitcast(F32)
            bank = psum_t.tile([P, PASSES, 2, P], F32, name="bank_t")
            for g in range(PASSES):
                for u in range(2):
                    nc.tensor.transpose(bank[:, g, u, :], words[:, 2 * P * g + u : 2 * P * (g + 1) : 2], ident[:])
            dst = x_packed[r][:, :, j].rearrange("p g m t -> p g (m t)").bitcast(F32)
            nc.scalar.copy(
                out=dst.rearrange("p g (m u) -> p g m u", u=2),
                in_=bank[:].rearrange("p g u m -> p g m u"),
            )

        def quantize_x_half(r, half):
            for g in range(PASSES):
                cols = slice(2 * half * P, 2 * (half + 1) * P)
                nc.vector.quantize_mx(
                    out=x_codes[:, r, g, cols].bitcast(E5M2),
                    scales=x_scales[:, r, g, cols],
                    in_=x_packed[r][:, g, 2 * half : 2 * half + 2].rearrange("p j m t -> p (j m t)"),
                )

        def quantize_x(r):
            nc.vector.quantize_mx(
                out=x_codes[:, r].rearrange("p g m -> p (g m)").bitcast(E5M2),
                scales=x_scales[:, r].rearrange("p g m -> p (g m)"),
                in_=x_packed[r][:].rearrange("p g j m t -> p (g j m t)"),
            )

        def pack_w(c, g, h, on_vector=False):
            if c not in w_packed:
                w_packed[c] = stage.tile([P, PASSES, HEADS, QK, PACK], BF16, align_bytes=64, name="w_packed")
            dst = w_packed[c][:, g, h].rearrange("p (n i) t -> p n t i", i=4)
            src = w_raw[c][:, g, h].rearrange("p t (n i) -> p n t i", i=4)
            if on_vector:
                nc.vector.tensor_copy(out=dst, in_=src)
            else:
                nc.scalar.copy(out=dst, in_=src)

        def transpose_x_group(r):
            for j in range(GROUP):
                transpose_x(r, j)

        def quantize_w(c, g):
            nc.vector.quantize_mx(
                out=w_codes[:, c, g].bitcast(E4M3),
                scales=w_scales[:, c, g],
                in_=w_packed[c][:, g].rearrange("p h n t -> p (h n t)"),
            )

        def quantize_w_set(c):
            nc.vector.quantize_mx(
                out=w_codes[:, c].rearrange("p g m -> p (g m)").bitcast(E4M3),
                scales=w_scales[:, c].rearrange("p g m -> p (g m)"),
                in_=w_packed[c][:].rearrange("p g h n t -> p (g h n t)"),
            )

        def widen_sin(engine, r0, r1):
            slots = slice(r0 * GROUP, r1 * GROUP)
            shape = [P, (r1 - r0) * GROUP * PAIRS, 2]
            engine.tensor_tensor(
                out=sin_signed[:, slots].rearrange("p s i e -> p (s i) e"),
                in0=sin_sb[:, slots].rearrange("p s i -> p (s i)").unsqueeze(2).to_broadcast(shape),
                in1=signs[:].unsqueeze(1).to_broadcast(shape),
                op=ALU.mult,
            )

        def widen_cos(r):
            slots = slice(r * GROUP, (r + 1) * GROUP)
            nc.scalar.copy(
                out=cos_twice[:, slots].rearrange("p s i e -> p (s i) e"),
                in_=cos_sb[:, slots].rearrange("p s i -> p (s i)").unsqueeze(2).to_broadcast([P, GROUP * PAIRS, 2]),
            )

        def transpose_tables(r):
            bank = psum_t.tile([P, PASSES, 2, P], F32, name="bank_t")
            flat = bank[:].rearrange("p g u m -> p (g u m)").bitcast(BF16)
            for a, table in enumerate((cos_twice, sin_signed)):
                for j in range(GROUP):
                    col = (a * GROUP + j) * P
                    nc.tensor.transpose(
                        flat[:, col : col + P], table[:, r * GROUP + j].rearrange("p i e -> p (i e)"), ident_bf[:]
                    )
            nc.scalar.copy(out=tables[:, r].rearrange("p a m -> p (a m)"), in_=flat)

        def unit(n):
            return n // (GROUPS * HALVES), n % (GROUPS * HALVES) // HALVES, n % HALVES

        def mx_pair(stationary, moving, fmt_s, fmt_m):
            banks = [psum_m.tile([P, 4 * P], F32, name="acc") for a in range(2)]
            for g in range(PASSES):
                for acc, (s_codes, s_scales), (m_codes, m_scales) in zip(banks, stationary, moving):
                    nc.tensor.matmul_mx(
                        out=acc[:],
                        lhsT=s_codes[:, g].bitcast(fmt_s),
                        lhsT_scale=s_scales[:, g],
                        rhs=m_codes[:, g].bitcast(fmt_m),
                        rhs_scale=m_scales[:, g],
                        start=(g == 0),
                        stop=(g == PASSES - 1),
                    )
            return banks

        q_banks = {}
        k_banks = {}
        q_result = {}
        k_parts = {}

        def multiply_q(n, out=0):
            c, r, half = unit(n)
            c += 2 * out
            cols = [slice((2 * half + a) * P, (2 * half + a + 1) * P) for a in range(2)]
            q_banks[n, out] = mx_pair(
                [(x_codes[:, r, :, s], x_scales[:, r, :, s]) for s in cols],
                [(w_codes[:, c], w_scales[:, c])] * 2,
                E5M2,
                E4M3,
            )

        def multiply_k(n):
            if n < TOKEN_K:
                return multiply_q(n, 1)
            c, r, half = unit(n)
            cols = [slice((2 * half + a) * QK, (2 * half + a + 1) * QK) for a in range(2)]
            k_banks[n] = mx_pair(
                [(w_codes[:, 2 + c, :, s], w_scales[:, 2 + c, :, s]) for s in cols],
                [(x_codes[:, r], x_scales[:, r])] * 2,
                E4M3,
                E5M2,
            )

        shape4 = [P, HEADS, PAIRS, 2]

        def rotate_q(n, out=0):
            c, r, half = unit(n)
            c += 2 * out
            if half == 0:
                q_result[n // 2, out] = prod.tile([P, HEADS, GROUP, QK], F32, name="q_result")
            result = q_result[n // 2, out]
            cos_part = prod.tile([P, 2, HEADS, QK], F32, name="q_cos_part")
            sin_part = prod.tile([P, 2, HEADS, QK], F32, name="q_sin_part")
            for a in (1, 0):
                s = r * GROUP + 2 * half + a
                pairs = q_banks[n, out][a][:].rearrange("p (h i e) -> p h i e", h=HEADS, e=2)
                nc.vector.tensor_tensor(
                    out=cos_part[:, a].rearrange("p h (i e) -> p h i e", e=2),
                    in0=pairs,
                    in1=cos_sb[:, s, :].unsqueeze(1).unsqueeze(3).to_broadcast(shape4),
                    op=ALU.mult,
                )
                nc.vector.tensor_tensor(
                    out=sin_part[:, a].rearrange("p h (i e) -> p h i e", e=2),
                    in0=pairs[:, :, :, ::-1],
                    in1=sin_signed[:, s].unsqueeze(1).to_broadcast(shape4),
                    op=ALU.mult,
                )
            nc.gpsimd.tensor_tensor(
                out=result[:, :, 2 * half : 2 * half + 2, :],
                in0=cos_part[:].rearrange("p j h c -> p h j c"),
                in1=sin_part[:].rearrange("p j h c -> p h j c"),
                op=ALU.subtract if out else ALU.add,
            )
            if n >= UNITS - 2:
                s0 = r * GROUP + 2 * half
                nc.sync.dma_start(out=set_output(c)[:, :, s0 : s0 + 2, :], in_=result[:, :, 2 * half : 2 * half + 2, :])
            elif half == 1:
                nc.sync.dma_start(out=set_output(c)[:, :, r * GROUP : (r + 1) * GROUP, :], in_=result[:])

        def products_k(n):
            if n < TOKEN_K:
                return rotate_q(n, 1)
            c, r, half = unit(n)
            cos_part = parts.tile([P, 2, GROUP * P], F32, name="k_cos_part")
            sin_part = parts.tile([P, 2, GROUP * P], F32, name="k_sin_part")
            k_parts[n] = (cos_part, sin_part)
            order = (0, 1) if n == UNITS - 1 else (1, 0)
            shared = gpsimd_banks(n)
            for a in order:
                bank = k_banks[n][a]
                if a >= 2 - shared:
                    nc.vector.tensor_tensor(out=sin_part[:, a], in0=bank[:], in1=tables[:, r, 1], op=ALU.mult)
                    nc.scalar.copy(out=cos_part[:, a], in_=bank[:])
                else:
                    nc.vector.tensor_tensor(out=cos_part[:, a], in0=bank[:], in1=tables[:, r, 0], op=ALU.mult)
                    nc.vector.tensor_tensor(out=sin_part[:, a], in0=bank[:], in1=tables[:, r, 1], op=ALU.mult)
            if shared:
                nc.gpsimd.tensor_tensor(
                    out=cos_part[:, 2 - shared :],
                    in0=cos_part[:, 2 - shared :],
                    in1=tables[:, r, 0].unsqueeze(1).to_broadcast([P, shared, GROUP * P]),
                    op=ALU.mult,
                )

        def finish_k(n):
            if n < TOKEN_K:
                return
            c, r, half = unit(n)
            cos_part, sin_part = k_parts[n]
            result = prod.tile([P, 2, GROUP * QK], F32, name="k_result")
            heads = set_output(2 + c)[:, 2 * half : 2 * half + 2, r * GROUP : (r + 1) * GROUP, :]
            heads = heads.rearrange("p h s c -> p h (s c)")
            for a in range(2):
                bank = psum_t.tile([P, PASSES, 2, P], F32, name="bank_t")
                flat = bank[:].rearrange("p g u m -> p (g u m)")
                for j in range(GROUP):
                    cols = slice(j * P, (j + 1) * P)
                    nc.tensor.matmul(
                        flat[:, cols], lhsT=sin_part[:, a, cols], rhs=swap[:], start=True, stop=False, is_transpose=True
                    )
                    nc.tensor.matmul(
                        flat[:, cols], lhsT=cos_part[:, a, cols], rhs=ident[:], start=False, stop=True, is_transpose=True
                    )
                nc.scalar.copy(out=result[:, a], in_=flat)
                if n == UNITS - 1:
                    nc.sync.dma_start(out=heads[:, a], in_=result[:, a])
            if n < UNITS - 1:
                nc.sync.dma_start(out=heads, in_=result[:])

        def gpsimd_banks(n):
            return 2 if n % 2 == 0 and 4 <= n < 14 else 0

        nc.sync.dma_start(out=sin_sb[:, : 2 * GROUP], in_=sin_hbm[:, : 2 * GROUP])
        load_w(0, 0)
        load_x(0, 0, 2)
        load_w(0, 1)
        nc.sync.dma_start(out=cos_sb[:, :GROUP], in_=cos_hbm[:, :GROUP])
        load_x(0, 2, GROUP)
        load_w(2, 0)
        load_w(2, 1)
        load_x(1, 0, 2)
        load_x(1, 2, GROUP)
        nc.sync.dma_start(out=sin_sb[:, 2 * GROUP :], in_=sin_hbm[:, 2 * GROUP :])
        nc.sync.dma_start(out=cos_sb[:, GROUP:], in_=cos_hbm[:, GROUP:])
        load_x(2, 0, GROUP)
        load_w(1, 0)
        load_w(1, 1)

        make_identity(nc, ident[:])
        make_identity(nc, ident_bf[:])
        nc.vector.memset(signs[:, 0:1], -1.0)
        nc.vector.memset(signs[:, 1:2], 1.0)
        nc.vector.tensor_copy(
            out=swap[:].rearrange("p (i e) -> p i e", e=2), in_=ident[:].rearrange("p (i e) -> p i e", e=2)[:, :, ::-1]
        )
        widen_sin(nc.vector, 0, 2)
        transpose_x(0, 0)
        transpose_x(0, 1)
        for h in range(HEADS):
            pack_w(0, 0, h, on_vector=True)
        quantize_w(0, 0)
        for h in range(HEADS):
            pack_w(0, 1, h, on_vector=h >= 1)
        quantize_x_half(0, 0)
        quantize_w(0, 1)
        transpose_x(0, 2)
        transpose_x(0, 3)
        multiply_q(0)
        for h in range(4):
            pack_w(2, 0, h, on_vector=True)
        quantize_x_half(0, 1)
        load_x(3, 0, GROUP)
        load_w(3, 0)
        load_w(3, 1)
        for g, h in [(g, h) for g in range(PASSES) for h in range(HEADS)][4:]:
            pack_w(2, g, h)

        steps = 2 * GROUPS
        for s in range(steps):
            n = 2 * s
            last = s == steps - 1
            multiply_q(n + 1)
            if s > 0:
                finish_k(n - 1)
            if s == 0:
                transpose_x_group(1)
            for c, g in {1: [(1, 1)], 2: [(3, 0)], 3: [(3, 1)]}.get(s, []):
                for h in range(HEADS):
                    pack_w(c, g, h)
            rotate_q(n)
            if s == 0:
                quantize_w_set(2)
            if s in (1, 2):
                quantize_x(s + 1)
            if s == 1:
                widen_sin(nc.gpsimd, 2, GROUPS)
            if s in (3, 4):
                quantize_w_set(2 * s - 5)
            if s > 0:
                multiply_k(n)
                multiply_k(n + 1)
            if s == 1:
                transpose_x(3, 0)
                transpose_x(3, 1)
            rotate_q(n + 1)
            if s == 0:
                multiply_k(n)
                multiply_k(n + 1)
                widen_cos(1)
                transpose_x(2, 0)
                transpose_x(2, 1)
            if last:
                finish_k(n - 2)
            products_k(n)
            if 0 < s < steps - 1:
                finish_k(n - 2)
            if s == 0:
                quantize_x(1)
            if not last:
                multiply_q(n + 2)
            if s == 0:
                transpose_x(2, 2)
                transpose_x(2, 3)
                transpose_tables(1)
                widen_cos(2)
                for h in range(HEADS):
                    pack_w(1, 0, h)
            if s == 1:
                transpose_x(3, 2)
                transpose_x(3, 3)
            if s in (1, 2):
                transpose_tables(s + 1)
            if s in (1, 2):
                widen_cos((s + 2) % GROUPS)
            if s == 3:
                transpose_tables(0)
            products_k(n + 1)
        finish_k(UNITS - 2)
        finish_k(UNITS - 1)
